import numpy as np
import ml_dtypes


def mxq(x, axis, fmt="e4m3"):
    dtype, down = {"e4m3": (ml_dtypes.float8_e4m3fn, 7), "e5m2": (ml_dtypes.float8_e5m2, 14)}[fmt]
    v = np.moveaxis(np.asarray(x, np.float32).astype(ml_dtypes.bfloat16).astype(np.float64), axis, -1)
    blocks = v.reshape(v.shape[:-1] + (-1, 32))
    amax = np.abs(blocks).max(-1, keepdims=True)
    byte = np.maximum(np.where(amax > 0, np.frexp(amax)[1] - 1 + 127, 0) - down, 1)
    scale = np.exp2(byte - 127.0)
    codes = (blocks / scale).astype(np.float32).astype(dtype).astype(np.float64)
    return np.moveaxis((codes * scale).reshape(v.shape), -1, axis)


WIDE = False


def mx_kscale(k):
    if not WIDE:
        return np.ones(k)
    levels = np.array([10, -10, 5, -5, 0])
    if k % 512:
        return np.exp2(np.random.permutation(np.resize(levels, k // 32))).repeat(32)
    a = np.empty((k // 512, 16))
    for p in range(k // 512):
        a[p, :8] = np.random.permutation(np.resize(levels, 8))
        for g in range(8):
            far = levels[np.abs(levels - a[p, g]) >= 10]
            a[p, g + 8] = far[np.random.randint(len(far))]
    return np.exp2(a.ravel()).repeat(32)


BF16 = ml_dtypes.bfloat16


def bf(x):
    return np.asarray(x, np.float32).astype(BF16)


def f64(x):
    return np.asarray(x).astype(np.float64)


B, S, HID, H, HKV, D, QB = 4, 2048, 1024, 2, 2, 64, 512
HALF = D // 2
ROPE_BASE = 10000.0


def rope_tables():
    inv_freq = 1.0 / (ROPE_BASE ** (np.arange(0, D, 2) / D))
    freqs = np.outer(np.arange(S), inv_freq)
    emb = np.concatenate([freqs, freqs], axis=-1)
    return np.cos(emb), np.sin(emb)


def rotate_half(t):
    return np.concatenate([-t[..., HALF:], t[..., :HALF]], axis=-1)


def apply_rope(t, cos, sin):
    return t * cos[None, None, :, :] + rotate_half(t) * sin[None, None, :, :]


def heads(y, n):
    return y.reshape(B, S, n, D).transpose(0, 2, 1, 3)


def setup_inputs():
    s = mx_kscale(HID)
    w = 1.0 / np.sqrt(HID)
    cos, sin = rope_tables()
    return {"x": bf(np.random.standard_normal((B, S, HID)) * s),
            "Wq": bf(np.random.standard_normal((H * D, HID)) * w / s[None, :]),
            "Wk": bf(np.random.standard_normal((HKV * D, HID)) * w / s[None, :]),
            "Wv": bf(np.random.standard_normal((HKV * D, HID)) * w / s[None, :]),
            "cos": bf(cos), "sin": bf(sin)}


def reference(x, Wq, Wk, Wv, cos, sin):
    xq = mxq(f64(x), 2, "e4m3")
    q = heads(xq @ mxq(f64(Wq), 1, "e4m3").T, H)
    k = heads(xq @ mxq(f64(Wk), 1, "e4m3").T, HKV)
    v = heads(xq @ mxq(f64(Wv), 1, "e4m3").T, HKV)
    c, sn = f64(cos), f64(sin)
    return apply_rope(q, c, sn), apply_rope(k, c, sn), v

@@ -1,0 +1,255 @@
+from contextlib import ExitStack
+
+import concourse.masks as masks
+import concourse.mybir as mybir
+
+F32 = mybir.dt.float32
+BF16 = mybir.dt.bfloat16
+U32 = mybir.dt.uint32
+U8 = mybir.dt.uint8
+FP8X4 = mybir.dt.float8_e4m3fn_x4
+MULT = mybir.AluOpType.mult
+ADD = mybir.AluOpType.add
+
+P = 128
+B, S, HID = 4, 2048, 1024
+HEADS, D = 2, 64
+HALF = D // 2
+GROUPS = 2 * HEADS
+
+K_PASS = 4 * P
+PASSES = HID // K_PASS
+WORDS = HID // 2
+BLOCKS = WORDS // P
+
+TILES = S // P
+CHUNK = 4
+RUN = 2
+RUNS = CHUNK // RUN
+CHUNKS_PER_BATCH = TILES // CHUNK
+NCHUNKS = B * CHUNKS_PER_BATCH
+
+X_BUFS = 8
+PREFETCH = X_BUFS - 1
+OUT_BUFS = 3
+
+LO, HI, V = 0, 1, 2
+
+FLOPS = 2 * B * S * HID * 3 * HEADS * D
+
+
+def tile_selfmha_pa_t_kernel(tc, x, Wq, Wk, Wv, cos, sin, out_0, out_1, out_2):
+    nc = tc.nc
+    with ExitStack() as ctx:
+        const = ctx.enter_context(tc.tile_pool(name="const", bufs=1))
+        xpool = ctx.enter_context(tc.tile_pool(name="xpool", bufs=X_BUFS))
+        quant = ctx.enter_context(tc.tile_pool(name="quant", bufs=3))
+        outs = ctx.enter_context(tc.tile_pool(name="outs", bufs=OUT_BUFS))
+        psum = ctx.enter_context(tc.psum_pool(name="psum", bufs=1))
+        ctx.enter_context(tc.manual_schedule())
+
+        w_raw = []
+        for n, w in enumerate((Wq, Wk, Wv)):
+            w_sb = const.tile([P, HID], BF16, name="w_raw%d" % n)
+            nc.sync.dma_start(out=w_sb[:], in_=w)
+            w_raw.append(w_sb)
+
+        x_sb = {}
+
+        def load_chunk(c, pieces):
+            b, cb = divmod(c, CHUNKS_PER_BATCH)
+            x_sb[c] = xpool.tile([P, CHUNK * HID], BF16, name="x_c")
+            rows = x[b].rearrange("(p j) k -> p (j k)", j=TILES)
+            width = CHUNK * HID // pieces
+            for i in range(pieces):
+                nc.sync.dma_start(
+                    out=x_sb[c][:, i * width : (i + 1) * width],
+                    in_=rows[:, cb * CHUNK * HID + i * width : cb * CHUNK * HID + (i + 1) * width],
+                )
+
+        cos_sb = const.tile([P, TILES, D], BF16, name="cos_sb")
+        sin_sb = const.tile([P, TILES, D], BF16, name="sin_sb")
+        load_chunk(0, CHUNK)
+        load_chunk(1, 1)
+        nc.sync.dma_start(out=cos_sb[:], in_=cos.rearrange("(p j) d -> p j d", j=TILES))
+        nc.sync.dma_start(out=sin_sb[:], in_=sin.rearrange("(p j) d -> p j d", j=TILES))
+        for c in range(2, PREFETCH):
+            load_chunk(c, 1)
+
+        ident = const.tile([P, P], F32, name="ident")
+        masks.make_identity(nc, ident[:])
+        nc.gpsimd.tensor_scalar_mul(out=sin_sb[:, :, 0:HALF], in0=sin_sb[:, :, 0:HALF], scalar1=-1.0)
+
+        def transpose_words(words):
+            bank = psum.tile([P, WORDS], F32, name="bank", tag="bank", bufs=3)
+            for blk in range(BLOCKS):
+                g, u = divmod(blk, 2)
+                every_2nd = slice(2 * g * P + u, 2 * (g + 1) * P, 2)
+                nc.tensor.transpose(
+                    bank[:, blk * P : (blk + 1) * P], words[:, every_2nd], ident[:]
+                )
+            return bank
+
+        def interleaved(bank):
+            return bank[:].rearrange("p (g u r) -> p g r u", g=PASSES, u=2)
+
+        w_grouped = const.tile([P, 3 * PASSES * P * 4], BF16, name="w_grouped", align_bytes=64)
+        w_codes = const.tile([P, 3 * PASSES * P], U32, name="w_codes", align_bytes=64)
+        w_scales = const.tile([P, 3 * PASSES * P], U8, name="w_scales", align_bytes=64)
+        w_words = w_grouped[:].bitcast(F32).rearrange(
+            "p (t g c u) -> p t g c u", t=3, g=PASSES, u=2
+        )
+        for n in range(2):
+            bank = transpose_words(w_raw[n][:].bitcast(F32))
+            halves = bank[:].rearrange(
+                "p (g u h f i) -> p g f h i u", g=PASSES, u=2, h=HEADS, f=2
+            )
+            for g in range(PASSES):
+                for f in (LO, HI):
+                    dst = w_words[:, f, g, n * HEADS * HALF : (n + 1) * HEADS * HALF, :]
+                    nc.vector.tensor_copy(
+                        out=dst.rearrange("p (h i) u -> p h i u", h=HEADS), in_=halves[:, g, f]
+                    )
+        bank = transpose_words(w_raw[2][:].bitcast(F32))
+        nc.vector.tensor_copy(out=w_words[:, V], in_=interleaved(bank))
+        for t in (LO, HI, V):
+            nc.vector.quantize_mx(
+                out=w_codes[:, t * PASSES * P : (t + 1) * PASSES * P].bitcast(FP8X4),
+                scales=w_scales[:, t * PASSES * P : (t + 1) * PASSES * P],
+                in_=w_grouped[:, t * PASSES * P * 4 : (t + 1) * PASSES * P * 4],
+            )
+
+        grouped = {}
+        codes = {}
+        scales = {}
+        sums = {}
+        rot = {}
+        qk_out = {}
+        v_out = {}
+
+        def transpose_run(c, r):
+            if r == 0:
+                grouped[c] = quant.tile([P, CHUNK * HID], BF16, name="grouped", align_bytes=64)
+            x_words = x_sb[c][:].bitcast(F32)
+            g_words = grouped[c][:].bitcast(F32)
+            for j in range(r * RUN, (r + 1) * RUN):
+                cols = slice(j * WORDS, (j + 1) * WORDS)
+                bank = transpose_words(x_words[:, cols])
+                nc.scalar.copy(
+                    out=g_words[:, cols].rearrange("p (g r u) -> p g r u", g=PASSES, u=2),
+                    in_=interleaved(bank),
+                )
+
+        def quantise_chunk(c):
+            codes[c] = quant.tile([P, CHUNK * PASSES * P], U32, name="codes", align_bytes=64)
+            scales[c] = quant.tile([P, CHUNK * PASSES * P], U8, name="scales", align_bytes=64)
+            for r in range(RUNS):
+                cols = slice(r * RUN * PASSES * P, (r + 1) * RUN * PASSES * P)
+                nc.vector.quantize_mx(
+                    out=codes[c][:, cols].bitcast(FP8X4),
+                    scales=scales[c][:, cols],
+                    in_=grouped[c][:, r * RUN * HID : (r + 1) * RUN * HID],
+                )
+
+        def multiply_run(c, r):
+            if r == 0:
+                lo = psum.tile([P, CHUNK * P], F32, name="lo", tag="lo", bufs=2)
+                hi = psum.tile([P, CHUNK * P], F32, name="hi", tag="hi", bufs=2)
+                vv = psum.tile([P, CHUNK * P], F32, name="vv", tag="vv", bufs=1)
+                sums[c] = (lo, hi, vv)
+            for j in range(r * RUN, (r + 1) * RUN):
+                for t in (LO, HI, V):
+                    for g in range(PASSES):
+                        xc = slice((j * PASSES + g) * P, (j * PASSES + g + 1) * P)
+                        wc = slice((t * PASSES + g) * P, (t * PASSES + g + 1) * P)
+                        nc.tensor.matmul_mx(
+                            out=sums[c][t][:, j * P : (j + 1) * P],
+                            lhsT=codes[c][:, xc].bitcast(FP8X4),
+                            lhsT_scale=scales[c][:, xc],
+                            rhs=w_codes[:, wc].bitcast(FP8X4),
+                            rhs_scale=w_scales[:, wc],
+                            start=(g == 0),
+                            stop=(g == PASSES - 1),
+                        )
+
+        def tiles_of(c):
+            cb = c % CHUNKS_PER_BATCH
+            return slice(cb * CHUNK, (cb + 1) * CHUNK)
+
+        def store(out_n, heads, c):
+            b, cb = divmod(c, CHUNKS_PER_BATCH)
+            rows = out_n[b].rearrange("h (p j) d -> p h j d", j=TILES)
+            if b == B - 1:
+                nc.sync.dma_start(out=rows[:, :, tiles_of(c), :], in_=heads[:, :, tiles_of(c), :])
+            elif cb == CHUNKS_PER_BATCH - 1:
+                nc.sync.dma_start(out=rows, in_=heads)
+
+        def copy_and_store_v(c):
+            b, cb = divmod(c, CHUNKS_PER_BATCH)
+            if cb == 0:
+                v_out[b] = outs.tile([P, HEADS, TILES, D], F32, name="v_out")
+            nc.scalar.copy(
+                out=v_out[b][:, :, tiles_of(c), :].rearrange("p h j d -> p j h d"),
+                in_=sums[c][V][:].rearrange("p (j h d) -> p j h d", j=CHUNK, h=HEADS),
+            )
+            store(out_2, v_out[b][:], c)
+
+        def table(tab, c, f):
+            rows = tab[:, tiles_of(c), f * HALF : (f + 1) * HALF]
+            return rows.unsqueeze(2).to_broadcast([P, CHUNK, GROUPS, HALF])
+
+        def rope_products(c):
+            b, cb = divmod(c, CHUNKS_PER_BATCH)
+            if cb == 0:
+                qk_out[b] = outs.tile([P, GROUPS, TILES, D], F32, name="qk_out")
+            rot[c] = quant.tile([P, GROUPS, CHUNK, D], F32, name="rot")
+            for f in (LO, HI):
+                cols = slice(f * HALF, (f + 1) * HALF)
+                same = sums[c][f][:].rearrange("p (j g i) -> p j g i", j=CHUNK, g=GROUPS)
+                other = sums[c][1 - f][:].rearrange("p (j g i) -> p j g i", j=CHUNK, g=GROUPS)
+                nc.vector.tensor_tensor(
+                    out=qk_out[b][:, :, tiles_of(c), cols].rearrange("p g j i -> p j g i"),
+                    in0=same,
+                    in1=table(cos_sb, c, f),
+                    op=MULT,
+                )
+                nc.vector.tensor_tensor(
+                    out=rot[c][:, :, :, cols].rearrange("p g j i -> p j g i"),
+                    in0=other,
+                    in1=table(sin_sb, c, f),
+                    op=MULT,
+                )
+
+        def rope_sum(engine, c, groups):
+            t_cos = qk_out[c // CHUNKS_PER_BATCH][:, groups, tiles_of(c), :]
+            engine.tensor_tensor(out=t_cos, in0=t_cos, in1=rot[c][:, groups], op=ADD)
+
+        def rope_sum_and_store(c):
+            qk = qk_out[c // CHUNKS_PER_BATCH]
+            q_heads, k_heads = slice(0, HEADS), slice(HEADS, GROUPS)
+            if c < NCHUNKS - 1:
+                rope_sum(nc.gpsimd, c, slice(0, GROUPS))
+                store(out_0, qk[:, q_heads], c)
+                store(out_1, qk[:, k_heads], c)
+            else:
+                rope_sum(nc.vector, c, q_heads)
+                store(out_0, qk[:, q_heads], c)
+                rope_sum(nc.vector, c, k_heads)
+                store(out_1, qk[:, k_heads], c)
+
+        for s in range(-3, NCHUNKS):
+            if s + 3 + PREFETCH < NCHUNKS:
+                load_chunk(s + 3 + PREFETCH, 1)
+            if s >= 0:
+                rope_products(s)
+            if 0 <= s + 2 < NCHUNKS:
+                quantise_chunk(s + 2)
+            for r in range(RUNS):
+                if s + 3 < NCHUNKS:
+                    transpose_run(s + 3, r)
+                if 0 <= s + 2 < NCHUNKS:
+                    multiply_run(s + 2, r)
+            if 0 <= s + 2 < NCHUNKS:
+                copy_and_store_v(s + 2)
+            if s >= 0:
+                rope_sum_and_store(s)

@@ -15,25 +15,24 @@ P = 128
 B, S, HID = 4, 2048, 1024
 HEADS, D = 2, 64
 HALF = D // 2
-GROUPS = 2 * HEADS
+ROTATED = 2 * HEADS
 
 K_PASS = 4 * P
 PASSES = HID // K_PASS
 WORDS = HID // 2
-BLOCKS = WORDS // P
+QK, V = 2 * P, P
 
 TILES = S // P
+PAIR = 2
+NPAIRS = B * TILES // PAIR
+PAIRS_PER_BATCH = TILES // PAIR
 CHUNK = 4
-RUN = 2
-RUNS = CHUNK // RUN
+PAIRS_PER_CHUNK = CHUNK // PAIR
+NCHUNKS = B * TILES // CHUNK
 CHUNKS_PER_BATCH = TILES // CHUNK
-NCHUNKS = B * CHUNKS_PER_BATCH
 
-X_BUFS = 8
-PREFETCH = X_BUFS - 1
+X_BUFS = 12
 OUT_BUFS = 3
-
-LO, HI, V = 0, 1, 2
 
 FLOPS = 2 * B * S * HID * 3 * HEADS * D
 
@@ -73,183 +72,198 @@ def tile_selfmha_pa_t_kernel(tc, x, Wq, Wk, Wv, cos, sin, out_0, out_1, out_2):
         load_chunk(1, 1)
         nc.sync.dma_start(out=cos_sb[:], in_=cos.rearrange("(p j) d -> p j d", j=TILES))
         nc.sync.dma_start(out=sin_sb[:], in_=sin.rearrange("(p j) d -> p j d", j=TILES))
-        for c in range(2, PREFETCH):
+        for c in range(2, X_BUFS):
             load_chunk(c, 1)
 
         ident = const.tile([P, P], F32, name="ident")
         masks.make_identity(nc, ident[:])
-        nc.gpsimd.tensor_scalar_mul(out=sin_sb[:, :, 0:HALF], in0=sin_sb[:, :, 0:HALF], scalar1=-1.0)
 
         def transpose_words(words):
             bank = psum.tile([P, WORDS], F32, name="bank", tag="bank", bufs=3)
-            for blk in range(BLOCKS):
-                g, u = divmod(blk, 2)
-                every_2nd = slice(2 * g * P + u, 2 * (g + 1) * P, 2)
-                nc.tensor.transpose(
-                    bank[:, blk * P : (blk + 1) * P], words[:, every_2nd], ident[:]
-                )
+            for g in range(PASSES):
+                for u in range(2):
+                    blk = 2 * g + u
+                    every_2nd = slice(2 * g * P + u, 2 * (g + 1) * P, 2)
+                    nc.tensor.transpose(
+                        bank[:, blk * P : (blk + 1) * P], words[:, every_2nd], ident[:]
+                    )
             return bank
 
         def interleaved(bank):
             return bank[:].rearrange("p (g u r) -> p g r u", g=PASSES, u=2)
 
-        w_grouped = const.tile([P, 3 * PASSES * P * 4], BF16, name="w_grouped", align_bytes=64)
-        w_codes = const.tile([P, 3 * PASSES * P], U32, name="w_codes", align_bytes=64)
-        w_scales = const.tile([P, 3 * PASSES * P], U8, name="w_scales", align_bytes=64)
-        w_words = w_grouped[:].bitcast(F32).rearrange(
-            "p (t g c u) -> p t g c u", t=3, g=PASSES, u=2
+        w_cols = PASSES * (QK + V)
+        w_grouped = const.tile([P, w_cols * 4], BF16, name="w_grouped", align_bytes=64)
+        w_codes = const.tile([P, w_cols], U32, name="w_codes", align_bytes=64)
+        w_scales = const.tile([P, w_cols], U8, name="w_scales", align_bytes=64)
+        w_words = w_grouped[:].bitcast(F32)
+        qk_words = w_words[:, 0 : PASSES * QK * 2].rearrange(
+            "p (g n r u) -> p g n r u", g=PASSES, n=2, u=2
         )
-        for n in range(2):
-            bank = transpose_words(w_raw[n][:].bitcast(F32))
-            halves = bank[:].rearrange(
-                "p (g u h f i) -> p g f h i u", g=PASSES, u=2, h=HEADS, f=2
-            )
-            for g in range(PASSES):
-                for f in (LO, HI):
-                    dst = w_words[:, f, g, n * HEADS * HALF : (n + 1) * HEADS * HALF, :]
-                    nc.vector.tensor_copy(
-                        out=dst.rearrange("p (h i) u -> p h i u", h=HEADS), in_=halves[:, g, f]
-                    )
-        bank = transpose_words(w_raw[2][:].bitcast(F32))
-        nc.vector.tensor_copy(out=w_words[:, V], in_=interleaved(bank))
-        for t in (LO, HI, V):
+        v_words = w_words[:, PASSES * QK * 2 :].rearrange("p (g r u) -> p g r u", g=PASSES, u=2)
+        nc.vector.tensor_copy(
+            out=qk_words[:, :, 0], in_=interleaved(transpose_words(w_raw[0][:].bitcast(F32)))
+        )
+        nc.scalar.copy(
+            out=qk_words[:, :, 1], in_=interleaved(transpose_words(w_raw[1][:].bitcast(F32)))
+        )
+        nc.vector.tensor_copy(
+            out=v_words, in_=interleaved(transpose_words(w_raw[2][:].bitcast(F32)))
+        )
+        for cols in (slice(0, PASSES * QK), slice(PASSES * QK, w_cols)):
             nc.vector.quantize_mx(
-                out=w_codes[:, t * PASSES * P : (t + 1) * PASSES * P].bitcast(FP8X4),
-                scales=w_scales[:, t * PASSES * P : (t + 1) * PASSES * P],
-                in_=w_grouped[:, t * PASSES * P * 4 : (t + 1) * PASSES * P * 4],
+                out=w_codes[:, cols].bitcast(FP8X4),
+                scales=w_scales[:, cols],
+                in_=w_grouped[:, cols.start * 4 : cols.stop * 4],
             )
 
         grouped = {}
         codes = {}
         scales = {}
-        sums = {}
+        qk_sums = {}
+        v_sums = {}
         rot = {}
         qk_out = {}
         v_out = {}
 
-        def transpose_run(c, r):
-            if r == 0:
-                grouped[c] = quant.tile([P, CHUNK * HID], BF16, name="grouped", align_bytes=64)
+        def transpose_pair(i):
+            grouped[i] = quant.tile([P, PAIR * HID], BF16, name="grouped", align_bytes=64)
+            c, first = divmod(i * PAIR, CHUNK)
             x_words = x_sb[c][:].bitcast(F32)
-            g_words = grouped[c][:].bitcast(F32)
-            for j in range(r * RUN, (r + 1) * RUN):
-                cols = slice(j * WORDS, (j + 1) * WORDS)
-                bank = transpose_words(x_words[:, cols])
+            g_words = grouped[i][:].bitcast(F32)
+            for j in range(PAIR):
+                bank = transpose_words(x_words[:, (first + j) * WORDS : (first + j + 1) * WORDS])
                 nc.scalar.copy(
-                    out=g_words[:, cols].rearrange("p (g r u) -> p g r u", g=PASSES, u=2),
+                    out=g_words[:, j * WORDS : (j + 1) * WORDS].rearrange(
+                        "p (g r u) -> p g r u", g=PASSES, u=2
+                    ),
                     in_=interleaved(bank),
                 )
 
-        def quantise_chunk(c):
-            codes[c] = quant.tile([P, CHUNK * PASSES * P], U32, name="codes", align_bytes=64)
-            scales[c] = quant.tile([P, CHUNK * PASSES * P], U8, name="scales", align_bytes=64)
-            for r in range(RUNS):
-                cols = slice(r * RUN * PASSES * P, (r + 1) * RUN * PASSES * P)
-                nc.vector.quantize_mx(
-                    out=codes[c][:, cols].bitcast(FP8X4),
-                    scales=scales[c][:, cols],
-                    in_=grouped[c][:, r * RUN * HID : (r + 1) * RUN * HID],
-                )
+        def quantise_pair(i):
+            codes[i] = quant.tile([P, PAIR * PASSES * P], U32, name="codes", align_bytes=64)
+            scales[i] = quant.tile([P, PAIR * PASSES * P], U8, name="scales", align_bytes=64)
+            nc.vector.quantize_mx(
+                out=codes[i][:].bitcast(FP8X4), scales=scales[i][:], in_=grouped[i][:]
+            )
 
-        def multiply_run(c, r):
-            if r == 0:
-                lo = psum.tile([P, CHUNK * P], F32, name="lo", tag="lo", bufs=2)
-                hi = psum.tile([P, CHUNK * P], F32, name="hi", tag="hi", bufs=2)
-                vv = psum.tile([P, CHUNK * P], F32, name="vv", tag="vv", bufs=1)
-                sums[c] = (lo, hi, vv)
-            for j in range(r * RUN, (r + 1) * RUN):
-                for t in (LO, HI, V):
+        def multiply_pair(i):
+            c, first = divmod(i * PAIR, CHUNK)
+            qk_sums[i] = psum.tile([P, PAIR * QK], F32, name="qk", tag="qk", bufs=3)
+            if first == 0:
+                v_sums[c] = psum.tile([P, CHUNK * V], F32, name="vv", tag="vv", bufs=2)
+            for j in range(PAIR):
+                qk_dst = qk_sums[i][:, j * QK : (j + 1) * QK]
+                v_dst = v_sums[c][:, (first + j) * V : (first + j + 1) * V]
+                for dst, width, base in ((qk_dst, QK, 0), (v_dst, V, PASSES * QK)):
                     for g in range(PASSES):
                         xc = slice((j * PASSES + g) * P, (j * PASSES + g + 1) * P)
-                        wc = slice((t * PASSES + g) * P, (t * PASSES + g + 1) * P)
+                        wc = slice(base + g * width, base + (g + 1) * width)
                         nc.tensor.matmul_mx(
-                            out=sums[c][t][:, j * P : (j + 1) * P],
-                            lhsT=codes[c][:, xc].bitcast(FP8X4),
-                            lhsT_scale=scales[c][:, xc],
+                            out=dst,
+                            lhsT=codes[i][:, xc].bitcast(FP8X4),
+                            lhsT_scale=scales[i][:, xc],
                             rhs=w_codes[:, wc].bitcast(FP8X4),
                             rhs_scale=w_scales[:, wc],
                             start=(g == 0),
                             stop=(g == PASSES - 1),
                         )
 
-        def tiles_of(c):
-            cb = c % CHUNKS_PER_BATCH
-            return slice(cb * CHUNK, (cb + 1) * CHUNK)
+        def store(out_n, heads, i, tiles):
+            rows = out_n[i // PAIRS_PER_BATCH].rearrange("h (p j) d -> p h j d", j=TILES)
+            nc.sync.dma_start(out=rows[:, :, tiles, :], in_=heads[:, :, tiles, :])
 
-        def store(out_n, heads, c):
-            b, cb = divmod(c, CHUNKS_PER_BATCH)
-            rows = out_n[b].rearrange("h (p j) d -> p h j d", j=TILES)
-            if b == B - 1:
-                nc.sync.dma_start(out=rows[:, :, tiles_of(c), :], in_=heads[:, :, tiles_of(c), :])
-            elif cb == CHUNKS_PER_BATCH - 1:
-                nc.sync.dma_start(out=rows, in_=heads)
+        def stored_after(i):
+            pairs = PAIRS_PER_CHUNK if i >= NPAIRS - PAIRS_PER_BATCH // 2 else PAIRS_PER_BATCH // 2
+            if (i + 1) % pairs:
+                return None
+            end = (i % PAIRS_PER_BATCH + 1) * PAIR
+            return slice(end - pairs * PAIR, end)
 
-        def copy_and_store_v(c):
+        def copy_and_store_v(i):
+            if (i + 1) % PAIRS_PER_CHUNK:
+                return
+            c = i // PAIRS_PER_CHUNK
             b, cb = divmod(c, CHUNKS_PER_BATCH)
             if cb == 0:
                 v_out[b] = outs.tile([P, HEADS, TILES, D], F32, name="v_out")
             nc.scalar.copy(
-                out=v_out[b][:, :, tiles_of(c), :].rearrange("p h j d -> p j h d"),
-                in_=sums[c][V][:].rearrange("p (j h d) -> p j h d", j=CHUNK, h=HEADS),
+                out=v_out[b][:, :, cb * CHUNK : (cb + 1) * CHUNK, :].rearrange("p h j d -> p j h d"),
+                in_=v_sums[c][:].rearrange("p (j h d) -> p j h d", j=CHUNK, h=HEADS),
             )
-            store(out_2, v_out[b][:], c)
+            tiles = stored_after(i)
+            if tiles is not None:
+                store(out_2, v_out[b][:], i, tiles)
 
-        def table(tab, c, f):
-            rows = tab[:, tiles_of(c), f * HALF : (f + 1) * HALF]
-            return rows.unsqueeze(2).to_broadcast([P, CHUNK, GROUPS, HALF])
+        def tiles_of(i):
+            first = i % PAIRS_PER_BATCH * PAIR
+            return slice(first, first + PAIR)
 
-        def rope_products(c):
-            b, cb = divmod(c, CHUNKS_PER_BATCH)
-            if cb == 0:
-                qk_out[b] = outs.tile([P, GROUPS, TILES, D], F32, name="qk_out")
-            rot[c] = quant.tile([P, GROUPS, CHUNK, D], F32, name="rot")
-            for f in (LO, HI):
-                cols = slice(f * HALF, (f + 1) * HALF)
-                same = sums[c][f][:].rearrange("p (j g i) -> p j g i", j=CHUNK, g=GROUPS)
-                other = sums[c][1 - f][:].rearrange("p (j g i) -> p j g i", j=CHUNK, g=GROUPS)
+        def table(tab, i, cols):
+            rows = tab[:, tiles_of(i), cols]
+            return rows.unsqueeze(2).to_broadcast([P, PAIR, ROTATED, cols.stop - cols.start])
+
+        def rope_products(i):
+            b, first = divmod(i, PAIRS_PER_BATCH)
+            if first == 0:
+                qk_out[b] = outs.tile([P, ROTATED, TILES, D], F32, name="qk_out")
+            rot[i] = quant.tile([P, PAIR, ROTATED, D], F32, name="rot")
+            t = qk_sums[i][:].rearrange("p (j g d) -> p j g d", j=PAIR, g=ROTATED)
+            lo, hi = slice(0, HALF), slice(HALF, D)
+            nc.vector.tensor_tensor(
+                out=qk_out[b][:, :, tiles_of(i), :].rearrange("p g j d -> p j g d"),
+                in0=t,
+                in1=table(cos_sb, i, slice(0, D)),
+                op=MULT,
+            )
+            for to, of in ((lo, hi), (hi, lo)):
                 nc.vector.tensor_tensor(
-                    out=qk_out[b][:, :, tiles_of(c), cols].rearrange("p g j i -> p j g i"),
-                    in0=same,
-                    in1=table(cos_sb, c, f),
+                    out=rot[i][:, :, :, to],
+                    in0=t[:, :, :, of],
+                    in1=table(sin_sb, i, to),
                     op=MULT,
                 )
-                nc.vector.tensor_tensor(
-                    out=rot[c][:, :, :, cols].rearrange("p g j i -> p j g i"),
-                    in0=other,
-                    in1=table(sin_sb, c, f),
-                    op=MULT,
-                )
 
-        def rope_sum(engine, c, groups):
-            t_cos = qk_out[c // CHUNKS_PER_BATCH][:, groups, tiles_of(c), :]
-            engine.tensor_tensor(out=t_cos, in0=t_cos, in1=rot[c][:, groups], op=ADD)
+        def rope_sum(engine, i, heads):
+            t_cos = qk_out[i // PAIRS_PER_BATCH][:, heads, tiles_of(i), :]
+            engine.tensor_tensor(
+                out=t_cos,
+                in0=t_cos,
+                in1=rot[i][:, :, heads, :].rearrange("p j g d -> p g j d"),
+                op=ADD,
+            )
 
-        def rope_sum_and_store(c):
-            qk = qk_out[c // CHUNKS_PER_BATCH]
-            q_heads, k_heads = slice(0, HEADS), slice(HEADS, GROUPS)
-            if c < NCHUNKS - 1:
-                rope_sum(nc.gpsimd, c, slice(0, GROUPS))
-                store(out_0, qk[:, q_heads], c)
-                store(out_1, qk[:, k_heads], c)
+        def rope_sum_and_store(i):
+            qk = qk_out[i // PAIRS_PER_BATCH]
+            q_heads, k_heads = slice(0, HEADS), slice(HEADS, ROTATED)
+            tiles = stored_after(i)
+            if i < NPAIRS - 1:
+                rope_sum(nc.gpsimd, i, slice(0, ROTATED))
+                if tiles is not None:
+                    store(out_0, qk[:, q_heads], i, tiles)
+                    store(out_1, qk[:, k_heads], i, tiles)
             else:
-                rope_sum(nc.vector, c, q_heads)
-                store(out_0, qk[:, q_heads], c)
-                rope_sum(nc.vector, c, k_heads)
-                store(out_1, qk[:, k_heads], c)
+                rope_sum(nc.vector, i, q_heads)
+                store(out_0, qk[:, q_heads], i, tiles)
+                rope_sum(nc.vector, i, k_heads)
+                store(out_1, qk[:, k_heads], i, tiles)
 
-        for s in range(-3, NCHUNKS):
-            if s + 3 + PREFETCH < NCHUNKS:
-                load_chunk(s + 3 + PREFETCH, 1)
+        for s in range(-4, NPAIRS):
+            if s == 0:
+                nc.vector.tensor_scalar_mul(
+                    out=sin_sb[:, :, 0:HALF], in0=sin_sb[:, :, 0:HALF], scalar1=-1.0
+                )
             if s >= 0:
                 rope_products(s)
-            if 0 <= s + 2 < NCHUNKS:
-                quantise_chunk(s + 2)
-            for r in range(RUNS):
-                if s + 3 < NCHUNKS:
-                    transpose_run(s + 3, r)
-                if 0 <= s + 2 < NCHUNKS:
-                    multiply_run(s + 2, r)
-            if 0 <= s + 2 < NCHUNKS:
+            if 0 <= s + 3 < NPAIRS:
+                quantise_pair(s + 3)
+            if s + 4 < NPAIRS:
+                transpose_pair(s + 4)
+                c, last = divmod(s + 4 + 1, PAIRS_PER_CHUNK)
+                if last == 0 and c - 1 + X_BUFS < NCHUNKS:
+                    load_chunk(c - 1 + X_BUFS, 1)
+            if 0 <= s + 2 < NPAIRS:
+                multiply_pair(s + 2)
                 copy_and_store_v(s + 2)
             if s >= 0:
                 rope_sum_and_store(s)

@@ -31,6 +31,7 @@ PAIRS_PER_CHUNK = CHUNK // PAIR
 NCHUNKS = B * TILES // CHUNK
 CHUNKS_PER_BATCH = TILES // CHUNK
 
+
 X_BUFS = 12
 OUT_BUFS = 3
 
@@ -78,15 +79,16 @@ def tile_selfmha_pa_t_kernel(tc, x, Wq, Wk, Wv, cos, sin, out_0, out_1, out_2):
         ident = const.tile([P, P], F32, name="ident")
         masks.make_identity(nc, ident[:])
 
-        def transpose_words(words):
+        def transpose_words(words, staged=None):
             bank = psum.tile([P, WORDS], F32, name="bank", tag="bank", bufs=3)
             for g in range(PASSES):
                 for u in range(2):
                     blk = 2 * g + u
-                    every_2nd = slice(2 * g * P + u, 2 * (g + 1) * P, 2)
-                    nc.tensor.transpose(
-                        bank[:, blk * P : (blk + 1) * P], words[:, every_2nd], ident[:]
-                    )
+                    if g == 0 and staged is not None:
+                        src = staged[:, u * P : (u + 1) * P]
+                    else:
+                        src = words[:, 2 * g * P + u : 2 * (g + 1) * P : 2]
+                    nc.tensor.transpose(bank[:, blk * P : (blk + 1) * P], src, ident[:])
             return bank
 
         def interleaved(bank):
@@ -117,6 +119,7 @@ def tile_selfmha_pa_t_kernel(tc, x, Wq, Wk, Wv, cos, sin, out_0, out_1, out_2):
                 in_=w_grouped[:, cols.start * 4 : cols.stop * 4],
             )
 
+        staged = {}
         grouped = {}
         codes = {}
         scales = {}
@@ -126,13 +129,31 @@ def tile_selfmha_pa_t_kernel(tc, x, Wq, Wk, Wv, cos, sin, out_0, out_1, out_2):
         qk_out = {}
         v_out = {}
 
+        def staged_tiles(i):
+            return 0 if i < 3 else 1 + i % 2
+
+        def stage_pair(i):
+            n = staged_tiles(i)
+            if n == 0:
+                return
+            staged[i] = quant.tile([P, n, 2 * P], F32, name="staged")
+            c, first = divmod(i * PAIR, CHUNK)
+            words = x_sb[c][:].bitcast(F32).rearrange("p (j g m u) -> p j g u m", j=CHUNK, g=PASSES, u=2)
+            nc.scalar.copy(
+                out=staged[i][:].rearrange("p j (u m) -> p j u m", u=2),
+                in_=words[:, first : first + n, 0],
+            )
+
         def transpose_pair(i):
             grouped[i] = quant.tile([P, PAIR * HID], BF16, name="grouped", align_bytes=64)
             c, first = divmod(i * PAIR, CHUNK)
             x_words = x_sb[c][:].bitcast(F32)
             g_words = grouped[i][:].bitcast(F32)
             for j in range(PAIR):
-                bank = transpose_words(x_words[:, (first + j) * WORDS : (first + j + 1) * WORDS])
+                bank = transpose_words(
+                    x_words[:, (first + j) * WORDS : (first + j + 1) * WORDS],
+                    staged[i][:, j] if j < staged_tiles(i) else None,
+                )
                 nc.scalar.copy(
                     out=g_words[:, j * WORDS : (j + 1) * WORDS].rearrange(
                         "p (g r u) -> p g r u", g=PASSES, u=2
@@ -248,7 +269,7 @@ def tile_selfmha_pa_t_kernel(tc, x, Wq, Wk, Wv, cos, sin, out_0, out_1, out_2):
                 rope_sum(nc.vector, i, k_heads)
                 store(out_1, qk[:, k_heads], i, tiles)
 
-        for s in range(-4, NPAIRS):
+        for s in range(-6, NPAIRS):
             if s == 0:
                 nc.vector.tensor_scalar_mul(
                     out=sin_sb[:, :, 0:HALF], in0=sin_sb[:, :, 0:HALF], scalar1=-1.0
@@ -257,11 +278,13 @@ def tile_selfmha_pa_t_kernel(tc, x, Wq, Wk, Wv, cos, sin, out_0, out_1, out_2):
                 rope_products(s)
             if 0 <= s + 3 < NPAIRS:
                 quantise_pair(s + 3)
-            if s + 4 < NPAIRS:
+            if 0 <= s + 4 < NPAIRS:
                 transpose_pair(s + 4)
                 c, last = divmod(s + 4 + 1, PAIRS_PER_CHUNK)
                 if last == 0 and c - 1 + X_BUFS < NCHUNKS:
                     load_chunk(c - 1 + X_BUFS, 1)
+            if s + 6 < NPAIRS:
+                stage_pair(s + 6)
             if 0 <= s + 2 < NPAIRS:
                 multiply_pair(s + 2)
                 copy_and_store_v(s + 2)

@@ -130,7 +130,7 @@ def tile_selfmha_pa_t_kernel(tc, x, Wq, Wk, Wv, cos, sin, out_0, out_1, out_2):
         v_out = {}
 
         def staged_tiles(i):
-            return 0 if i < 3 else 1 + i % 2
+            return 0 if i < 3 else 1
 
         def stage_pair(i):
             n = staged_tiles(i)

from contextlib import ExitStack

import concourse.masks as masks
import concourse.mybir as mybir

F32 = mybir.dt.float32
BF16 = mybir.dt.bfloat16
U32 = mybir.dt.uint32
U8 = mybir.dt.uint8
FP8X4 = mybir.dt.float8_e4m3fn_x4
MULT = mybir.AluOpType.mult
ADD = mybir.AluOpType.add

P = 128
B, S, HID = 4, 2048, 1024
HEADS, D = 2, 64
HALF = D // 2
ROTATED = 2 * HEADS

K_PASS = 4 * P
PASSES = HID // K_PASS
WORDS = HID // 2
QK, V = 2 * P, P

TILES = S // P
PAIR = 2
NPAIRS = B * TILES // PAIR
PAIRS_PER_BATCH = TILES // PAIR
CHUNK = 4
PAIRS_PER_CHUNK = CHUNK // PAIR
NCHUNKS = B * TILES // CHUNK
CHUNKS_PER_BATCH = TILES // CHUNK


X_BUFS = 12
OUT_BUFS = 3

FLOPS = 2 * B * S * HID * 3 * HEADS * D


def tile_selfmha_pa_t_kernel(tc, x, Wq, Wk, Wv, cos, sin, out_0, out_1, out_2):
    nc = tc.nc
    with ExitStack() as ctx:
        const = ctx.enter_context(tc.tile_pool(name="const", bufs=1))
        xpool = ctx.enter_context(tc.tile_pool(name="xpool", bufs=X_BUFS))
        quant = ctx.enter_context(tc.tile_pool(name="quant", bufs=3))
        outs = ctx.enter_context(tc.tile_pool(name="outs", bufs=OUT_BUFS))
        psum = ctx.enter_context(tc.psum_pool(name="psum", bufs=1))
        ctx.enter_context(tc.manual_schedule())

        w_raw = []
        for n, w in enumerate((Wq, Wk, Wv)):
            w_sb = const.tile([P, HID], BF16, name="w_raw%d" % n)
            nc.sync.dma_start(out=w_sb[:], in_=w)
            w_raw.append(w_sb)

        x_sb = {}

        def load_chunk(c, pieces):
            b, cb = divmod(c, CHUNKS_PER_BATCH)
            x_sb[c] = xpool.tile([P, CHUNK * HID], BF16, name="x_c")
            rows = x[b].rearrange("(p j) k -> p (j k)", j=TILES)
            width = CHUNK * HID // pieces
            for i in range(pieces):
                nc.sync.dma_start(
                    out=x_sb[c][:, i * width : (i + 1) * width],
                    in_=rows[:, cb * CHUNK * HID + i * width : cb * CHUNK * HID + (i + 1) * width],
                )

        cos_sb = const.tile([P, TILES, D], BF16, name="cos_sb")
        sin_sb = const.tile([P, TILES, D], BF16, name="sin_sb")
        load_chunk(0, CHUNK)
        load_chunk(1, 1)
        nc.sync.dma_start(out=cos_sb[:], in_=cos.rearrange("(p j) d -> p j d", j=TILES))
        nc.sync.dma_start(out=sin_sb[:], in_=sin.rearrange("(p j) d -> p j d", j=TILES))
        for c in range(2, X_BUFS):
            load_chunk(c, 1)

        ident = const.tile([P, P], F32, name="ident")
        masks.make_identity(nc, ident[:])

        def transpose_words(words, staged=None):
            bank = psum.tile([P, WORDS], F32, name="bank", tag="bank", bufs=3)
            for g in range(PASSES):
                for u in range(2):
                    blk = 2 * g + u
                    if g == 0 and staged is not None:
                        src = staged[:, u * P : (u + 1) * P]
                    else:
                        src = words[:, 2 * g * P + u : 2 * (g + 1) * P : 2]
                    nc.tensor.transpose(bank[:, blk * P : (blk + 1) * P], src, ident[:])
            return bank

        def interleaved(bank):
            return bank[:].rearrange("p (g u r) -> p g r u", g=PASSES, u=2)

        w_cols = PASSES * (QK + V)
        w_grouped = const.tile([P, w_cols * 4], BF16, name="w_grouped", align_bytes=64)
        w_codes = const.tile([P, w_cols], U32, name="w_codes", align_bytes=64)
        w_scales = const.tile([P, w_cols], U8, name="w_scales", align_bytes=64)
        w_words = w_grouped[:].bitcast(F32)
        qk_words = w_words[:, 0 : PASSES * QK * 2].rearrange(
            "p (g n r u) -> p g n r u", g=PASSES, n=2, u=2
        )
        v_words = w_words[:, PASSES * QK * 2 :].rearrange("p (g r u) -> p g r u", g=PASSES, u=2)
        nc.vector.tensor_copy(
            out=qk_words[:, :, 0], in_=interleaved(transpose_words(w_raw[0][:].bitcast(F32)))
        )
        nc.scalar.copy(
            out=qk_words[:, :, 1], in_=interleaved(transpose_words(w_raw[1][:].bitcast(F32)))
        )
        nc.vector.tensor_copy(
            out=v_words, in_=interleaved(transpose_words(w_raw[2][:].bitcast(F32)))
        )
        for cols in (slice(0, PASSES * QK), slice(PASSES * QK, w_cols)):
            nc.vector.quantize_mx(
                out=w_codes[:, cols].bitcast(FP8X4),
                scales=w_scales[:, cols],
                in_=w_grouped[:, cols.start * 4 : cols.stop * 4],
            )

        staged = {}
        grouped = {}
        codes = {}
        scales = {}
        qk_sums = {}
        v_sums = {}
        rot = {}
        qk_out = {}
        v_out = {}

        def staged_tiles(i):
            return 0 if i < 3 else 1

        def stage_pair(i):
            n = staged_tiles(i)
            if n == 0:
                return
            staged[i] = quant.tile([P, n, 2 * P], F32, name="staged")
            c, first = divmod(i * PAIR, CHUNK)
            words = x_sb[c][:].bitcast(F32).rearrange("p (j g m u) -> p j g u m", j=CHUNK, g=PASSES, u=2)
            nc.scalar.copy(
                out=staged[i][:].rearrange("p j (u m) -> p j u m", u=2),
                in_=words[:, first : first + n, 0],
            )

        def transpose_pair(i):
            grouped[i] = quant.tile([P, PAIR * HID], BF16, name="grouped", align_bytes=64)
            c, first = divmod(i * PAIR, CHUNK)
            x_words = x_sb[c][:].bitcast(F32)
            g_words = grouped[i][:].bitcast(F32)
            for j in range(PAIR):
                bank = transpose_words(
                    x_words[:, (first + j) * WORDS : (first + j + 1) * WORDS],
                    staged[i][:, j] if j < staged_tiles(i) else None,
                )
                nc.scalar.copy(
                    out=g_words[:, j * WORDS : (j + 1) * WORDS].rearrange(
                        "p (g r u) -> p g r u", g=PASSES, u=2
                    ),
                    in_=interleaved(bank),
                )

        def quantise_pair(i):
            codes[i] = quant.tile([P, PAIR * PASSES * P], U32, name="codes", align_bytes=64)
            scales[i] = quant.tile([P, PAIR * PASSES * P], U8, name="scales", align_bytes=64)
            nc.vector.quantize_mx(
                out=codes[i][:].bitcast(FP8X4), scales=scales[i][:], in_=grouped[i][:]
            )

        def multiply_pair(i):
            c, first = divmod(i * PAIR, CHUNK)
            qk_sums[i] = psum.tile([P, PAIR * QK], F32, name="qk", tag="qk", bufs=3)
            if first == 0:
                v_sums[c] = psum.tile([P, CHUNK * V], F32, name="vv", tag="vv", bufs=2)
            for j in range(PAIR):
                qk_dst = qk_sums[i][:, j * QK : (j + 1) * QK]
                v_dst = v_sums[c][:, (first + j) * V : (first + j + 1) * V]
                for dst, width, base in ((qk_dst, QK, 0), (v_dst, V, PASSES * QK)):
                    for g in range(PASSES):
                        xc = slice((j * PASSES + g) * P, (j * PASSES + g + 1) * P)
                        wc = slice(base + g * width, base + (g + 1) * width)
                        nc.tensor.matmul_mx(
                            out=dst,
                            lhsT=codes[i][:, xc].bitcast(FP8X4),
                            lhsT_scale=scales[i][:, xc],
                            rhs=w_codes[:, wc].bitcast(FP8X4),
                            rhs_scale=w_scales[:, wc],
                            start=(g == 0),
                            stop=(g == PASSES - 1),
                        )

        def store(out_n, heads, i, tiles):
            rows = out_n[i // PAIRS_PER_BATCH].rearrange("h (p j) d -> p h j d", j=TILES)
            nc.sync.dma_start(out=rows[:, :, tiles, :], in_=heads[:, :, tiles, :])

        def stored_after(i):
            pairs = PAIRS_PER_CHUNK if i >= NPAIRS - PAIRS_PER_BATCH // 2 else PAIRS_PER_BATCH // 2
            if (i + 1) % pairs:
                return None
            end = (i % PAIRS_PER_BATCH + 1) * PAIR
            return slice(end - pairs * PAIR, end)

        def copy_and_store_v(i):
            if (i + 1) % PAIRS_PER_CHUNK:
                return
            c = i // PAIRS_PER_CHUNK
            b, cb = divmod(c, CHUNKS_PER_BATCH)
            if cb == 0:
                v_out[b] = outs.tile([P, HEADS, TILES, D], F32, name="v_out")
            nc.scalar.copy(
                out=v_out[b][:, :, cb * CHUNK : (cb + 1) * CHUNK, :].rearrange("p h j d -> p j h d"),
                in_=v_sums[c][:].rearrange("p (j h d) -> p j h d", j=CHUNK, h=HEADS),
            )
            tiles = stored_after(i)
            if tiles is not None:
                store(out_2, v_out[b][:], i, tiles)

        def tiles_of(i):
            first = i % PAIRS_PER_BATCH * PAIR
            return slice(first, first + PAIR)

        def table(tab, i, cols):
            rows = tab[:, tiles_of(i), cols]
            return rows.unsqueeze(2).to_broadcast([P, PAIR, ROTATED, cols.stop - cols.start])

        def rope_products(i):
            b, first = divmod(i, PAIRS_PER_BATCH)
            if first == 0:
                qk_out[b] = outs.tile([P, ROTATED, TILES, D], F32, name="qk_out")
            rot[i] = quant.tile([P, PAIR, ROTATED, D], F32, name="rot")
            t = qk_sums[i][:].rearrange("p (j g d) -> p j g d", j=PAIR, g=ROTATED)
            lo, hi = slice(0, HALF), slice(HALF, D)
            nc.vector.tensor_tensor(
                out=qk_out[b][:, :, tiles_of(i), :].rearrange("p g j d -> p j g d"),
                in0=t,
                in1=table(cos_sb, i, slice(0, D)),
                op=MULT,
            )
            for to, of in ((lo, hi), (hi, lo)):
                nc.vector.tensor_tensor(
                    out=rot[i][:, :, :, to],
                    in0=t[:, :, :, of],
                    in1=table(sin_sb, i, to),
                    op=MULT,
                )

        def rope_sum(engine, i, heads):
            t_cos = qk_out[i // PAIRS_PER_BATCH][:, heads, tiles_of(i), :]
            engine.tensor_tensor(
                out=t_cos,
                in0=t_cos,
                in1=rot[i][:, :, heads, :].rearrange("p j g d -> p g j d"),
                op=ADD,
            )

        def rope_sum_and_store(i):
            qk = qk_out[i // PAIRS_PER_BATCH]
            q_heads, k_heads = slice(0, HEADS), slice(HEADS, ROTATED)
            tiles = stored_after(i)
            if i < NPAIRS - 1:
                rope_sum(nc.gpsimd, i, slice(0, ROTATED))
                if tiles is not None:
                    store(out_0, qk[:, q_heads], i, tiles)
                    store(out_1, qk[:, k_heads], i, tiles)
            else:
                rope_sum(nc.vector, i, q_heads)
                store(out_0, qk[:, q_heads], i, tiles)
                rope_sum(nc.vector, i, k_heads)
                store(out_1, qk[:, k_heads], i, tiles)

        for s in range(-6, NPAIRS):
            if s == 0:
                nc.vector.tensor_scalar_mul(
                    out=sin_sb[:, :, 0:HALF], in0=sin_sb[:, :, 0:HALF], scalar1=-1.0
                )
            if s >= 0:
                rope_products(s)
            if 0 <= s + 3 < NPAIRS:
                quantise_pair(s + 3)
            if 0 <= s + 4 < NPAIRS:
                transpose_pair(s + 4)
                c, last = divmod(s + 4 + 1, PAIRS_PER_CHUNK)
                if last == 0 and c - 1 + X_BUFS < NCHUNKS:
                    load_chunk(c - 1 + X_BUFS, 1)
            if s + 6 < NPAIRS:
                stage_pair(s + 6)
            if 0 <= s + 2 < NPAIRS:
                multiply_pair(s + 2)
                copy_and_store_v(s + 2)
            if s >= 0:
                rope_sum_and_store(s)
